import numpy as np
import ml_dtypes

BF16 = ml_dtypes.bfloat16


def bf(x):
    return np.asarray(x, np.float32).astype(BF16)


def f32(x):
    return np.asarray(x, np.float32)


def f64(x):
    return np.asarray(x).astype(np.float64)


def striped(idx):
    return np.tile(idx.reshape(-1, 16).T, (8, 1))


C, S, N, F = 256, 512, 128, 256
KEEP = 0.0625


def setup_inputs():
    u = np.random.random_sample((N, N)) * (np.random.random_sample((N, N)) < KEEP)
    a = np.triu(u) + np.triu(u, 1).T
    return {"x": bf(np.random.standard_normal((F, N))), "w1": bf(np.random.standard_normal((F, C)) / np.sqrt(F)), "b1": f32(0.1 * np.random.standard_normal((C, 1))), "adj": bf(a), "base": f32(np.random.standard_normal((C, S))), "offs": striped(np.random.permutation(S)[:N])}


def reference(x, w1, b1, adj, base, offs):
    idx = offs[:16].T.reshape(-1)
    a = f64(adj)
    dinv = 1.0 / np.sqrt(a.sum(axis=1) + 1.0)
    hs = (f64(w1).T @ f64(x) + f64(b1)) * dinv[None, :]
    agg = hs @ a.T + hs
    out = f64(base).copy()
    out[:, idx] = agg * dinv[None, :]
    return out

@@ -1,0 +1,69 @@
+import concourse.mybir as mybir
+from concourse.masks import make_identity
+
+BF16, F32, U16 = mybir.dt.bfloat16, mybir.dt.float32, mybir.dt.uint16
+MULT, ADD = mybir.AluOpType.mult, mybir.AluOpType.add
+SQRT = mybir.ActivationFunctionType.Sqrt
+
+P = 128
+FEATURES, CHANNELS, NODES, STORE = 256, 256, 128, 512
+F_TILES = FEATURES // P
+C_BLOCKS = CHANNELS // P
+
+FLOPS = 2 * FEATURES * CHANNELS * NODES + 2 * NODES * NODES * CHANNELS
+
+
+def tile_gcnlayer_kernel(tc, x, w1, b1, adj, base, offs, out):
+    nc = tc.nc
+    with (
+        tc.tile_pool(name="held", bufs=1) as held,
+        tc.psum_pool(name="psum", bufs=1) as psum,
+    ):
+        adj_sb = held.tile([P, NODES], BF16, name="adj_sb")
+        x_sb = held.tile([P, F_TILES, NODES], BF16, name="x_sb")
+        w1_sb = held.tile([P, F_TILES, CHANNELS], BF16, name="w1_sb")
+        bias_rows = held.tile([P, CHANNELS], F32, name="bias_rows")
+        offsets = held.tile([P, NODES // 16], U16, name="offsets")
+        windows = [held.tile([P, STORE], F32, name=f"window{b}") for b in range(C_BLOCKS)]
+
+        nc.sync.dma_start(adj_sb[:], adj)
+        nc.scalar.dma_start(w1_sb[:], w1.rearrange("(p t) c -> p t c", t=F_TILES))
+        nc.sync.dma_start(x_sb[:], x.rearrange("(p t) k -> p t k", t=F_TILES))
+        nc.scalar.dma_start(bias_rows[:], b1.rearrange("c o -> (c o)").partition_broadcast(P))
+        nc.sync.dma_start(offsets[:], offs)
+        nc.sync.dma_start(windows[0][:], base[0:P, :])
+        nc.scalar.dma_start(windows[1][:], base[P : 2 * P, :])
+
+        ones = held.tile([P, P], BF16, name="ones")
+        nc.vector.memset(ones[:], 1.0)
+        identity = held.tile([P, P], BF16, name="identity")
+        make_identity(nc, identity[:])
+
+        sums = psum.tile([P, NODES + 1], F32, name="sums")
+        nc.tensor.matmul(sums[:, 0:NODES], ones[:], adj_sb[:], start=True, stop=True)
+        nc.tensor.matmul(sums[:, NODES : NODES + 1], adj_sb[:], ones[:, 0:1], start=True, stop=True)
+        root = held.tile([P, NODES + 1], F32, name="root")
+        nc.scalar.activation(root[:], sums[:], SQRT, bias=1.0)
+        dinv = held.tile([P, NODES + 1], F32, name="dinv")
+        nc.vector.reciprocal(dinv[:], root[:])
+        dinv_row = dinv[:, 0:NODES]
+        dinv_own = dinv[:, NODES : NODES + 1]
+
+        bias_scaled = held.tile([P, CHANNELS], F32, name="bias_scaled")
+        nc.vector.tensor_scalar_mul(bias_scaled[:], bias_rows[:], dinv_own)
+        h_t = psum.tile([P, CHANNELS], F32, name="h_t")
+        for t in range(F_TILES):
+            nc.tensor.matmul(h_t[:], x_sb[:, t, :], w1_sb[:, t, :], start=(t == 0), stop=(t == F_TILES - 1))
+        hs_t = held.tile([P, CHANNELS], BF16, name="hs_t")
+        nc.vector.scalar_tensor_tensor(hs_t[:], h_t[:], dinv_own, bias_scaled[:], MULT, ADD)
+
+        for b in range(C_BLOCKS):
+            hs_block = hs_t[:, b * P : (b + 1) * P]
+            agg = psum.tile([P, NODES], F32, name=f"agg{b}")
+            nc.tensor.matmul(agg[:], hs_block, adj_sb[:], start=True, stop=False)
+            nc.tensor.matmul(agg[:], hs_block, identity[:], start=False, stop=True)
+            agg_sb = held.tile([P, NODES], F32, name=f"agg_sb{b}")
+            nc.scalar.copy(agg_sb[:], agg[:])
+            nc.vector.tensor_tensor(windows[b][:].indirect(offsets[:]), agg_sb[:], dinv_row, MULT)
+            store_queue = nc.sync if b == 0 else nc.scalar
+            store_queue.dma_start(out[b * P : (b + 1) * P, :], windows[b][:])

@@ -3,7 +3,7 @@ from concourse.masks import make_identity
 
 BF16, F32, U16 = mybir.dt.bfloat16, mybir.dt.float32, mybir.dt.uint16
 MULT, ADD = mybir.AluOpType.mult, mybir.AluOpType.add
-SQRT = mybir.ActivationFunctionType.Sqrt
+RSQRT_OF_ABS = mybir.ActivationFunctionType.Abs_reciprocal_sqrt
 
 P = 128
 FEATURES, CHANNELS, NODES, STORE = 256, 256, 128, 512
@@ -42,10 +42,8 @@ def tile_gcnlayer_kernel(tc, x, w1, b1, adj, base, offs, out):
         sums = psum.tile([P, NODES + 1], F32, name="sums")
         nc.tensor.matmul(sums[:, 0:NODES], ones[:], adj_sb[:], start=True, stop=True)
         nc.tensor.matmul(sums[:, NODES : NODES + 1], adj_sb[:], ones[:, 0:1], start=True, stop=True)
-        root = held.tile([P, NODES + 1], F32, name="root")
-        nc.scalar.activation(root[:], sums[:], SQRT, bias=1.0)
         dinv = held.tile([P, NODES + 1], F32, name="dinv")
-        nc.vector.reciprocal(dinv[:], root[:])
+        nc.scalar.activation(dinv[:], sums[:], RSQRT_OF_ABS, bias=1.0)
         dinv_row = dinv[:, 0:NODES]
         dinv_own = dinv[:, NODES : NODES + 1]
 

@@ -49,17 +49,19 @@ def tile_gcnlayer_kernel(tc, x, w1, b1, adj, base, offs, out):
 
         bias_scaled = held.tile([P, CHANNELS], F32, name="bias_scaled")
         nc.vector.tensor_scalar_mul(bias_scaled[:], bias_rows[:], dinv_own)
-        h_t = psum.tile([P, CHANNELS], F32, name="h_t")
-        for t in range(F_TILES):
-            nc.tensor.matmul(h_t[:], x_sb[:, t, :], w1_sb[:, t, :], start=(t == 0), stop=(t == F_TILES - 1))
-        hs_t = held.tile([P, CHANNELS], BF16, name="hs_t")
-        nc.vector.scalar_tensor_tensor(hs_t[:], h_t[:], dinv_own, bias_scaled[:], MULT, ADD)
+        hs_t = []
+        for b in range(C_BLOCKS):
+            block = slice(b * P, (b + 1) * P)
+            h_t = psum.tile([P, P], F32, name=f"h_t{b}")
+            for t in range(F_TILES):
+                nc.tensor.matmul(h_t[:], x_sb[:, t, :], w1_sb[:, t, block], start=(t == 0), stop=(t == F_TILES - 1))
+            hs_t.append(held.tile([P, P], BF16, name=f"hs_t{b}"))
+            nc.vector.scalar_tensor_tensor(hs_t[b][:], h_t[:], dinv_own, bias_scaled[:, block], MULT, ADD)
 
         for b in range(C_BLOCKS):
-            hs_block = hs_t[:, b * P : (b + 1) * P]
             agg = psum.tile([P, NODES], F32, name=f"agg{b}")
-            nc.tensor.matmul(agg[:], hs_block, adj_sb[:], start=True, stop=False)
-            nc.tensor.matmul(agg[:], hs_block, identity[:], start=False, stop=True)
+            nc.tensor.matmul(agg[:], hs_t[b][:], adj_sb[:], start=True, stop=False)
+            nc.tensor.matmul(agg[:], hs_t[b][:], identity[:], start=False, stop=True)
             agg_sb = held.tile([P, NODES], F32, name=f"agg_sb{b}")
             nc.scalar.copy(agg_sb[:], agg[:])
             nc.vector.tensor_tensor(windows[b][:].indirect(offsets[:]), agg_sb[:], dinv_row, MULT)

@@ -31,8 +31,8 @@ def tile_gcnlayer_kernel(tc, x, w1, b1, adj, base, offs, out):
         nc.sync.dma_start(x_sb[:], x.rearrange("(p t) k -> p t k", t=F_TILES))
         nc.scalar.dma_start(bias_rows[:], b1.rearrange("c o -> (c o)").partition_broadcast(P))
         nc.sync.dma_start(offsets[:], offs)
-        nc.sync.dma_start(windows[0][:], base[0:P, :])
-        nc.scalar.dma_start(windows[1][:], base[P : 2 * P, :])
+        for b in range(C_BLOCKS):
+            nc.sync.dma_start(windows[b][:], base[b * P : (b + 1) * P, :])
 
         ones = held.tile([P, P], BF16, name="ones")
         nc.vector.memset(ones[:], 1.0)

@@ -2,7 +2,7 @@ import concourse.mybir as mybir
 from concourse.masks import make_identity
 
 BF16, F32, U16 = mybir.dt.bfloat16, mybir.dt.float32, mybir.dt.uint16
-MULT, ADD = mybir.AluOpType.mult, mybir.AluOpType.add
+MULT, SUBTRACT = mybir.AluOpType.mult, mybir.AluOpType.subtract
 RSQRT_OF_ABS = mybir.ActivationFunctionType.Abs_reciprocal_sqrt
 
 P = 128
@@ -22,14 +22,14 @@ def tile_gcnlayer_kernel(tc, x, w1, b1, adj, base, offs, out):
         adj_sb = held.tile([P, NODES], BF16, name="adj_sb")
         x_sb = held.tile([P, F_TILES, NODES], BF16, name="x_sb")
         w1_sb = held.tile([P, F_TILES, CHANNELS], BF16, name="w1_sb")
-        bias_rows = held.tile([P, CHANNELS], F32, name="bias_rows")
+        bias_row = held.tile([1, CHANNELS], F32, name="bias_row")
         offsets = held.tile([P, NODES // 16], U16, name="offsets")
         windows = [held.tile([P, STORE], F32, name=f"window{b}") for b in range(C_BLOCKS)]
 
         nc.sync.dma_start(adj_sb[:], adj)
-        nc.scalar.dma_start(w1_sb[:], w1.rearrange("(p t) c -> p t c", t=F_TILES))
+        nc.scalar.dma_start(bias_row[:], b1.rearrange("c o -> o c"))
         nc.sync.dma_start(x_sb[:], x.rearrange("(p t) k -> p t k", t=F_TILES))
-        nc.scalar.dma_start(bias_rows[:], b1.rearrange("c o -> (c o)").partition_broadcast(P))
+        nc.scalar.dma_start(w1_sb[:], w1.rearrange("(p t) c -> p t c", t=F_TILES))
         nc.sync.dma_start(offsets[:], offs)
         for b in range(C_BLOCKS):
             nc.sync.dma_start(windows[b][:], base[b * P : (b + 1) * P, :])
@@ -47,16 +47,20 @@ def tile_gcnlayer_kernel(tc, x, w1, b1, adj, base, offs, out):
         dinv_row = dinv[:, 0:NODES]
         dinv_own = dinv[:, NODES : NODES + 1]
 
-        bias_scaled = held.tile([P, CHANNELS], F32, name="bias_scaled")
-        nc.vector.tensor_scalar_mul(bias_scaled[:], bias_rows[:], dinv_own)
+        bias_hi = held.tile([1, CHANNELS], BF16, name="bias_hi")
+        nc.vector.tensor_copy(bias_hi[:], bias_row[:])
+        bias_lo = held.tile([1, CHANNELS], BF16, name="bias_lo")
+        nc.vector.tensor_tensor(bias_lo[:], bias_row[:], bias_hi[:], SUBTRACT)
         hs_t = []
         for b in range(C_BLOCKS):
             block = slice(b * P, (b + 1) * P)
             h_t = psum.tile([P, P], F32, name=f"h_t{b}")
             for t in range(F_TILES):
-                nc.tensor.matmul(h_t[:], x_sb[:, t, :], w1_sb[:, t, block], start=(t == 0), stop=(t == F_TILES - 1))
+                nc.tensor.matmul(h_t[:], x_sb[:, t, :], w1_sb[:, t, block], start=(t == 0), stop=False)
+            nc.tensor.matmul(h_t[:], ones[0:1, :], bias_hi[:, block], start=False, stop=False)
+            nc.tensor.matmul(h_t[:], ones[0:1, :], bias_lo[:, block], start=False, stop=True)
             hs_t.append(held.tile([P, P], BF16, name=f"hs_t{b}"))
-            nc.vector.scalar_tensor_tensor(hs_t[b][:], h_t[:], dinv_own, bias_scaled[:, block], MULT, ADD)
+            nc.vector.tensor_scalar_mul(hs_t[b][:], h_t[:], dinv_own)
 
         for b in range(C_BLOCKS):
             agg = psum.tile([P, NODES], F32, name=f"agg{b}")

@@ -9,6 +9,8 @@ P = 128
 FEATURES, CHANNELS, NODES, STORE = 256, 256, 128, 512
 F_TILES = FEATURES // P
 C_BLOCKS = CHANNELS // P
+BANK = 512
+WARM_UP_MATMULS = 3
 
 FLOPS = 2 * FEATURES * CHANNELS * NODES + 2 * NODES * NODES * CHANNELS
 
@@ -34,13 +36,16 @@ def tile_gcnlayer_kernel(tc, x, w1, b1, adj, base, offs, out):
         for b in range(C_BLOCKS):
             nc.sync.dma_start(windows[b][:], base[b * P : (b + 1) * P, :])
 
-        ones = held.tile([P, P], BF16, name="ones")
+        ones = held.tile([P, BANK], BF16, name="ones")
         nc.vector.memset(ones[:], 1.0)
+        warm_up = psum.tile([P, BANK], F32, name="warm_up")
+        for i in range(WARM_UP_MATMULS):
+            nc.tensor.matmul(warm_up[:], ones[:, 0:P], ones[:], start=True, stop=True)
         identity = held.tile([P, P], BF16, name="identity")
         make_identity(nc, identity[:])
 
         sums = psum.tile([P, NODES + 1], F32, name="sums")
-        nc.tensor.matmul(sums[:, 0:NODES], ones[:], adj_sb[:], start=True, stop=True)
+        nc.tensor.matmul(sums[:, 0:NODES], ones[:, 0:P], adj_sb[:], start=True, stop=True)
         nc.tensor.matmul(sums[:, NODES : NODES + 1], adj_sb[:], ones[:, 0:1], start=True, stop=True)
         dinv = held.tile([P, NODES + 1], F32, name="dinv")
         nc.scalar.activation(dinv[:], sums[:], RSQRT_OF_ABS, bias=1.0)
@@ -57,8 +62,8 @@ def tile_gcnlayer_kernel(tc, x, w1, b1, adj, base, offs, out):
             h_t = psum.tile([P, P], F32, name=f"h_t{b}")
             for t in range(F_TILES):
                 nc.tensor.matmul(h_t[:], x_sb[:, t, :], w1_sb[:, t, block], start=(t == 0), stop=False)
-            nc.tensor.matmul(h_t[:], ones[0:1, :], bias_hi[:, block], start=False, stop=False)
-            nc.tensor.matmul(h_t[:], ones[0:1, :], bias_lo[:, block], start=False, stop=True)
+            nc.tensor.matmul(h_t[:], ones[0:1, 0:P], bias_hi[:, block], start=False, stop=False)
+            nc.tensor.matmul(h_t[:], ones[0:1, 0:P], bias_lo[:, block], start=False, stop=True)
             hs_t.append(held.tile([P, P], BF16, name=f"hs_t{b}"))
             nc.vector.tensor_scalar_mul(hs_t[b][:], h_t[:], dinv_own)
 

@@ -2,7 +2,7 @@ import concourse.mybir as mybir
 from concourse.masks import make_identity
 
 BF16, F32, U16 = mybir.dt.bfloat16, mybir.dt.float32, mybir.dt.uint16
-MULT, SUBTRACT = mybir.AluOpType.mult, mybir.AluOpType.subtract
+MULT = mybir.AluOpType.mult
 RSQRT_OF_ABS = mybir.ActivationFunctionType.Abs_reciprocal_sqrt
 
 P = 128
@@ -41,6 +41,8 @@ def tile_gcnlayer_kernel(tc, x, w1, b1, adj, base, offs, out):
         warm_up = psum.tile([P, BANK], F32, name="warm_up")
         for i in range(WARM_UP_MATMULS):
             nc.tensor.matmul(warm_up[:], ones[:, 0:P], ones[:], start=True, stop=True)
+        ones_row = held.tile([1, NODES], F32, name="ones_row")
+        nc.vector.memset(ones_row[:], 1.0)
         identity = held.tile([P, P], BF16, name="identity")
         make_identity(nc, identity[:])
 
@@ -52,18 +54,13 @@ def tile_gcnlayer_kernel(tc, x, w1, b1, adj, base, offs, out):
         dinv_row = dinv[:, 0:NODES]
         dinv_own = dinv[:, NODES : NODES + 1]
 
-        bias_hi = held.tile([1, CHANNELS], BF16, name="bias_hi")
-        nc.vector.tensor_copy(bias_hi[:], bias_row[:])
-        bias_lo = held.tile([1, CHANNELS], BF16, name="bias_lo")
-        nc.vector.tensor_tensor(bias_lo[:], bias_row[:], bias_hi[:], SUBTRACT)
         hs_t = []
         for b in range(C_BLOCKS):
             block = slice(b * P, (b + 1) * P)
             h_t = psum.tile([P, P], F32, name=f"h_t{b}")
+            nc.tensor.matmul(h_t[:], ones_row[:], bias_row[:, block], start=True, stop=False)
             for t in range(F_TILES):
-                nc.tensor.matmul(h_t[:], x_sb[:, t, :], w1_sb[:, t, block], start=(t == 0), stop=False)
-            nc.tensor.matmul(h_t[:], ones[0:1, 0:P], bias_hi[:, block], start=False, stop=False)
-            nc.tensor.matmul(h_t[:], ones[0:1, 0:P], bias_lo[:, block], start=False, stop=True)
+                nc.tensor.matmul(h_t[:], x_sb[:, t, :], w1_sb[:, t, block], start=False, stop=(t == F_TILES - 1))
             hs_t.append(held.tile([P, P], BF16, name=f"hs_t{b}"))
             nc.vector.tensor_scalar_mul(hs_t[b][:], h_t[:], dinv_own)
 

@@ -2,7 +2,7 @@ import concourse.mybir as mybir
 from concourse.masks import make_identity
 
 BF16, F32, U16 = mybir.dt.bfloat16, mybir.dt.float32, mybir.dt.uint16
-MULT = mybir.AluOpType.mult
+MULT, SUBTRACT = mybir.AluOpType.mult, mybir.AluOpType.subtract
 RSQRT_OF_ABS = mybir.ActivationFunctionType.Abs_reciprocal_sqrt
 
 P = 128
@@ -41,8 +41,6 @@ def tile_gcnlayer_kernel(tc, x, w1, b1, adj, base, offs, out):
         warm_up = psum.tile([P, BANK], F32, name="warm_up")
         for i in range(WARM_UP_MATMULS):
             nc.tensor.matmul(warm_up[:], ones[:, 0:P], ones[:], start=True, stop=True)
-        ones_row = held.tile([1, NODES], F32, name="ones_row")
-        nc.vector.memset(ones_row[:], 1.0)
         identity = held.tile([P, P], BF16, name="identity")
         make_identity(nc, identity[:])
 
@@ -54,13 +52,20 @@ def tile_gcnlayer_kernel(tc, x, w1, b1, adj, base, offs, out):
         dinv_row = dinv[:, 0:NODES]
         dinv_own = dinv[:, NODES : NODES + 1]
 
+        bias_parts = held.tile([P, 2, CHANNELS], BF16, name="bias_parts")
+        nc.vector.memset(bias_parts[:], 0.0)
+        for b in range(C_BLOCKS):
+            block = slice(b * P, (b + 1) * P)
+            nc.vector.tensor_copy(bias_parts[0:1, 0, block], bias_row[:, block])
+            nc.vector.tensor_tensor(bias_parts[0:1, 1, block], bias_row[:, block], bias_parts[0:1, 0, block], SUBTRACT)
         hs_t = []
         for b in range(C_BLOCKS):
             block = slice(b * P, (b + 1) * P)
             h_t = psum.tile([P, P], F32, name=f"h_t{b}")
-            nc.tensor.matmul(h_t[:], ones_row[:], bias_row[:, block], start=True, stop=False)
             for t in range(F_TILES):
-                nc.tensor.matmul(h_t[:], x_sb[:, t, :], w1_sb[:, t, block], start=False, stop=(t == F_TILES - 1))
+                nc.tensor.matmul(h_t[:], x_sb[:, t, :], w1_sb[:, t, block], start=(t == 0), stop=False)
+            nc.tensor.matmul(h_t[:], ones[:, 0:P], bias_parts[:, 0, block], start=False, stop=False)
+            nc.tensor.matmul(h_t[:], ones[:, 0:P], bias_parts[:, 1, block], start=False, stop=True)
             hs_t.append(held.tile([P, P], BF16, name=f"hs_t{b}"))
             nc.vector.tensor_scalar_mul(hs_t[b][:], h_t[:], dinv_own)
 

@@ -4,13 +4,13 @@ from concourse.masks import make_identity
 BF16, F32, U16 = mybir.dt.bfloat16, mybir.dt.float32, mybir.dt.uint16
 MULT, SUBTRACT = mybir.AluOpType.mult, mybir.AluOpType.subtract
 RSQRT_OF_ABS = mybir.ActivationFunctionType.Abs_reciprocal_sqrt
+ALONG_ROW = mybir.AxisListType.X
 
 P = 128
 FEATURES, CHANNELS, NODES, STORE = 256, 256, 128, 512
 F_TILES = FEATURES // P
 C_BLOCKS = CHANNELS // P
-BANK = 512
-WARM_UP_MATMULS = 3
+WARM_UP_MATMULS = 12
 
 FLOPS = 2 * FEATURES * CHANNELS * NODES + 2 * NODES * NODES * CHANNELS
 
@@ -28,46 +28,51 @@ def tile_gcnlayer_kernel(tc, x, w1, b1, adj, base, offs, out):
         offsets = held.tile([P, NODES // 16], U16, name="offsets")
         windows = [held.tile([P, STORE], F32, name=f"window{b}") for b in range(C_BLOCKS)]
 
-        nc.sync.dma_start(adj_sb[:], adj)
-        nc.scalar.dma_start(bias_row[:], b1.rearrange("c o -> o c"))
-        nc.sync.dma_start(x_sb[:], x.rearrange("(p t) k -> p t k", t=F_TILES))
         nc.scalar.dma_start(w1_sb[:], w1.rearrange("(p t) c -> p t c", t=F_TILES))
+        nc.sync.dma_start(bias_row[:], b1.rearrange("c o -> o c"))
+        nc.sync.dma_start(adj_sb[:], adj)
+        nc.sync.dma_start(x_sb[:], x.rearrange("(p t) k -> p t k", t=F_TILES))
         nc.sync.dma_start(offsets[:], offs)
         for b in range(C_BLOCKS):
             nc.sync.dma_start(windows[b][:], base[b * P : (b + 1) * P, :])
 
-        ones = held.tile([P, BANK], BF16, name="ones")
-        nc.vector.memset(ones[:], 1.0)
-        warm_up = psum.tile([P, BANK], F32, name="warm_up")
+        idle_work = held.tile([P, P], BF16, name="idle_work")
+        nc.vector.memset(idle_work[:], 0.0)
+        warm_up = psum.tile([P, P], F32, name="warm_up")
         for i in range(WARM_UP_MATMULS):
-            nc.tensor.matmul(warm_up[:], ones[:, 0:P], ones[:], start=True, stop=True)
+            nc.tensor.matmul(warm_up[:], idle_work[:], idle_work[:], start=True, stop=True)
         identity = held.tile([P, P], BF16, name="identity")
         make_identity(nc, identity[:])
-
-        sums = psum.tile([P, NODES + 1], F32, name="sums")
-        nc.tensor.matmul(sums[:, 0:NODES], ones[:, 0:P], adj_sb[:], start=True, stop=True)
-        nc.tensor.matmul(sums[:, NODES : NODES + 1], adj_sb[:], ones[:, 0:1], start=True, stop=True)
-        dinv = held.tile([P, NODES + 1], F32, name="dinv")
-        nc.scalar.activation(dinv[:], sums[:], RSQRT_OF_ABS, bias=1.0)
-        dinv_row = dinv[:, 0:NODES]
-        dinv_own = dinv[:, NODES : NODES + 1]
-
+        ones = held.tile([P, P], BF16, name="ones")
+        nc.vector.memset(ones[:], 1.0)
         bias_parts = held.tile([P, 2, CHANNELS], BF16, name="bias_parts")
         nc.vector.memset(bias_parts[:], 0.0)
+
+        degree_own = held.tile([P, 1], F32, name="degree_own")
+        nc.vector.reduce_sum(degree_own[:], adj_sb[:], axis=ALONG_ROW)
+        dinv_own = held.tile([P, 1], F32, name="dinv_own")
+        nc.scalar.activation(dinv_own[:], degree_own[:], RSQRT_OF_ABS, bias=1.0)
+        sums_row = psum.tile([P, NODES], F32, name="sums_row")
+        nc.tensor.matmul(sums_row[:], ones[:], adj_sb[:], start=True, stop=True)
+        dinv_row = held.tile([P, NODES], F32, name="dinv_row")
+        nc.scalar.activation(dinv_row[:], sums_row[:], RSQRT_OF_ABS, bias=1.0)
+
         for b in range(C_BLOCKS):
             block = slice(b * P, (b + 1) * P)
             nc.vector.tensor_copy(bias_parts[0:1, 0, block], bias_row[:, block])
             nc.vector.tensor_tensor(bias_parts[0:1, 1, block], bias_row[:, block], bias_parts[0:1, 0, block], SUBTRACT)
+        h_t = [psum.tile([P, P], F32, name=f"h_t{b}") for b in range(C_BLOCKS)]
+        for b in range(C_BLOCKS):
+            block = slice(b * P, (b + 1) * P)
+            nc.tensor.matmul(h_t[b][:], ones[:], bias_parts[:, 0, block], start=True, stop=False)
+            nc.tensor.matmul(h_t[b][:], ones[:], bias_parts[:, 1, block], start=False, stop=False)
         hs_t = []
         for b in range(C_BLOCKS):
             block = slice(b * P, (b + 1) * P)
-            h_t = psum.tile([P, P], F32, name=f"h_t{b}")
             for t in range(F_TILES):
-                nc.tensor.matmul(h_t[:], x_sb[:, t, :], w1_sb[:, t, block], start=(t == 0), stop=False)
-            nc.tensor.matmul(h_t[:], ones[:, 0:P], bias_parts[:, 0, block], start=False, stop=False)
-            nc.tensor.matmul(h_t[:], ones[:, 0:P], bias_parts[:, 1, block], start=False, stop=True)
+                nc.tensor.matmul(h_t[b][:], x_sb[:, t, :], w1_sb[:, t, block], start=False, stop=(t == F_TILES - 1))
             hs_t.append(held.tile([P, P], BF16, name=f"hs_t{b}"))
-            nc.vector.tensor_scalar_mul(hs_t[b][:], h_t[:], dinv_own)
+            nc.vector.tensor_scalar_mul(hs_t[b][:], h_t[b][:], dinv_own[:])
 
         for b in range(C_BLOCKS):
             agg = psum.tile([P, NODES], F32, name=f"agg{b}")
@@ -75,6 +80,6 @@ def tile_gcnlayer_kernel(tc, x, w1, b1, adj, base, offs, out):
             nc.tensor.matmul(agg[:], hs_t[b][:], identity[:], start=False, stop=True)
             agg_sb = held.tile([P, NODES], F32, name=f"agg_sb{b}")
             nc.scalar.copy(agg_sb[:], agg[:])
-            nc.vector.tensor_tensor(windows[b][:].indirect(offsets[:]), agg_sb[:], dinv_row, MULT)
+            nc.vector.tensor_tensor(windows[b][:].indirect(offsets[:]), agg_sb[:], dinv_row[:], MULT)
             store_queue = nc.sync if b == 0 else nc.scalar
             store_queue.dma_start(out[b * P : (b + 1) * P, :], windows[b][:])

@@ -24,12 +24,12 @@ def tile_gcnlayer_kernel(tc, x, w1, b1, adj, base, offs, out):
         adj_sb = held.tile([P, NODES], BF16, name="adj_sb")
         x_sb = held.tile([P, F_TILES, NODES], BF16, name="x_sb")
         w1_sb = held.tile([P, F_TILES, CHANNELS], BF16, name="w1_sb")
-        bias_row = held.tile([1, CHANNELS], F32, name="bias_row")
+        bias_cols = held.tile([P, C_BLOCKS], F32, name="bias_cols")
         offsets = held.tile([P, NODES // 16], U16, name="offsets")
         windows = [held.tile([P, STORE], F32, name=f"window{b}") for b in range(C_BLOCKS)]
 
         nc.scalar.dma_start(w1_sb[:], w1.rearrange("(p t) c -> p t c", t=F_TILES))
-        nc.sync.dma_start(bias_row[:], b1.rearrange("c o -> o c"))
+        nc.sync.dma_start(bias_cols[:], b1.rearrange("(b p) o -> p (b o)", p=P))
         nc.sync.dma_start(adj_sb[:], adj)
         nc.sync.dma_start(x_sb[:], x.rearrange("(p t) k -> p t k", t=F_TILES))
         nc.sync.dma_start(offsets[:], offs)
@@ -45,34 +45,35 @@ def tile_gcnlayer_kernel(tc, x, w1, b1, adj, base, offs, out):
         make_identity(nc, identity[:])
         ones = held.tile([P, P], BF16, name="ones")
         nc.vector.memset(ones[:], 1.0)
-        bias_parts = held.tile([P, 2, CHANNELS], BF16, name="bias_parts")
-        nc.vector.memset(bias_parts[:], 0.0)
 
         degree_own = held.tile([P, 1], F32, name="degree_own")
         nc.vector.reduce_sum(degree_own[:], adj_sb[:], axis=ALONG_ROW)
         dinv_own = held.tile([P, 1], F32, name="dinv_own")
         nc.scalar.activation(dinv_own[:], degree_own[:], RSQRT_OF_ABS, bias=1.0)
+
+        bias_high = held.tile([P, C_BLOCKS], BF16, name="bias_high")
+        nc.vector.tensor_copy(bias_high[:], bias_cols[:])
+        bias_low = held.tile([P, C_BLOCKS], BF16, name="bias_low")
+        nc.vector.tensor_tensor(bias_low[:], bias_cols[:], bias_high[:], SUBTRACT)
+        def scaled_features(b):
+            block = slice(b * P, (b + 1) * P)
+            h_t = psum.tile([P, P], F32, name=f"h_t{b}")
+            nc.tensor.matmul(h_t[:], bias_high[:, b : b + 1].to_broadcast([P, P]), identity[:], start=True, stop=False)
+            nc.tensor.matmul(h_t[:], bias_low[:, b : b + 1].to_broadcast([P, P]), identity[:], start=False, stop=False)
+            for t in range(F_TILES):
+                nc.tensor.matmul(h_t[:], x_sb[:, t, :], w1_sb[:, t, block], start=False, stop=(t == F_TILES - 1))
+            hs_t_block = held.tile([P, P], BF16, name=f"hs_t{b}")
+            nc.vector.tensor_scalar_mul(hs_t_block[:], h_t[:], dinv_own[:])
+            return hs_t_block
+
+        hs_t = [scaled_features(0)]
+
         sums_row = psum.tile([P, NODES], F32, name="sums_row")
         nc.tensor.matmul(sums_row[:], ones[:], adj_sb[:], start=True, stop=True)
         dinv_row = held.tile([P, NODES], F32, name="dinv_row")
         nc.scalar.activation(dinv_row[:], sums_row[:], RSQRT_OF_ABS, bias=1.0)
 
-        for b in range(C_BLOCKS):
-            block = slice(b * P, (b + 1) * P)
-            nc.vector.tensor_copy(bias_parts[0:1, 0, block], bias_row[:, block])
-            nc.vector.tensor_tensor(bias_parts[0:1, 1, block], bias_row[:, block], bias_parts[0:1, 0, block], SUBTRACT)
-        h_t = [psum.tile([P, P], F32, name=f"h_t{b}") for b in range(C_BLOCKS)]
-        for b in range(C_BLOCKS):
-            block = slice(b * P, (b + 1) * P)
-            nc.tensor.matmul(h_t[b][:], ones[:], bias_parts[:, 0, block], start=True, stop=False)
-            nc.tensor.matmul(h_t[b][:], ones[:], bias_parts[:, 1, block], start=False, stop=False)
-        hs_t = []
-        for b in range(C_BLOCKS):
-            block = slice(b * P, (b + 1) * P)
-            for t in range(F_TILES):
-                nc.tensor.matmul(h_t[b][:], x_sb[:, t, :], w1_sb[:, t, block], start=False, stop=(t == F_TILES - 1))
-            hs_t.append(held.tile([P, P], BF16, name=f"hs_t{b}"))
-            nc.vector.tensor_scalar_mul(hs_t[b][:], h_t[b][:], dinv_own[:])
+        hs_t.extend(scaled_features(b) for b in range(1, C_BLOCKS))
 
         for b in range(C_BLOCKS):
             agg = psum.tile([P, NODES], F32, name=f"agg{b}")

@@ -10,7 +10,7 @@ P = 128
 FEATURES, CHANNELS, NODES, STORE = 256, 256, 128, 512
 F_TILES = FEATURES // P
 C_BLOCKS = CHANNELS // P
-WARM_UP_MATMULS = 12
+WARM_UP_MATMULS = 16
 
 FLOPS = 2 * FEATURES * CHANNELS * NODES + 2 * NODES * NODES * CHANNELS
 
@@ -36,11 +36,11 @@ def tile_gcnlayer_kernel(tc, x, w1, b1, adj, base, offs, out):
         for b in range(C_BLOCKS):
             nc.sync.dma_start(windows[b][:], base[b * P : (b + 1) * P, :])
 
-        idle_work = held.tile([P, P], BF16, name="idle_work")
-        nc.vector.memset(idle_work[:], 0.0)
+        idle_work = held.tile([P, 1], BF16, name="idle_work")
+        nc.gpsimd.memset(idle_work[:], 0.0)
         warm_up = psum.tile([P, P], F32, name="warm_up")
         for i in range(WARM_UP_MATMULS):
-            nc.tensor.matmul(warm_up[:], idle_work[:], idle_work[:], start=True, stop=True)
+            nc.tensor.matmul(warm_up[:], idle_work[:].to_broadcast([P, P]), idle_work[:].to_broadcast([P, P]), start=True, stop=True)
         identity = held.tile([P, P], BF16, name="identity")
         make_identity(nc, identity[:])
         ones = held.tile([P, P], BF16, name="ones")

@@ -80,7 +80,10 @@ def tile_gcnlayer_kernel(tc, x, w1, b1, adj, base, offs, out):
             nc.tensor.matmul(agg[:], hs_t[b][:], adj_sb[:], start=True, stop=False)
             nc.tensor.matmul(agg[:], hs_t[b][:], identity[:], start=False, stop=True)
             agg_sb = held.tile([P, NODES], F32, name=f"agg_sb{b}")
-            nc.scalar.copy(agg_sb[:], agg[:])
+            if b == 0:
+                nc.vector.tensor_copy(agg_sb[:], agg[:])
+            else:
+                nc.scalar.copy(agg_sb[:], agg[:])
             nc.vector.tensor_tensor(windows[b][:].indirect(offsets[:]), agg_sb[:], dinv_row[:], MULT)
-            store_queue = nc.sync if b == 0 else nc.scalar
+            store_queue = nc.sync if b == C_BLOCKS - 1 else nc.scalar
             store_queue.dma_start(out[b * P : (b + 1) * P, :], windows[b][:])

@@ -32,9 +32,9 @@ def tile_gcnlayer_kernel(tc, x, w1, b1, adj, base, offs, out):
         nc.sync.dma_start(bias_cols[:], b1.rearrange("(b p) o -> p (b o)", p=P))
         nc.sync.dma_start(adj_sb[:], adj)
         nc.sync.dma_start(x_sb[:], x.rearrange("(p t) k -> p t k", t=F_TILES))
-        nc.sync.dma_start(offsets[:], offs)
         for b in range(C_BLOCKS):
             nc.sync.dma_start(windows[b][:], base[b * P : (b + 1) * P, :])
+        nc.sync.dma_start(offsets[:], offs)
 
         idle_work = held.tile([P, 1], BF16, name="idle_work")
         nc.gpsimd.memset(idle_work[:], 0.0)

@@ -23,12 +23,13 @@ def tile_gcnlayer_kernel(tc, x, w1, b1, adj, base, offs, out):
     ):
         adj_sb = held.tile([P, NODES], BF16, name="adj_sb")
         x_sb = held.tile([P, F_TILES, NODES], BF16, name="x_sb")
-        w1_sb = held.tile([P, F_TILES, CHANNELS], BF16, name="w1_sb")
+        w1_sb = [held.tile([P, F_TILES, P], BF16, name=f"w1_sb{b}") for b in range(C_BLOCKS)]
         bias_cols = held.tile([P, C_BLOCKS], F32, name="bias_cols")
         offsets = held.tile([P, NODES // 16], U16, name="offsets")
         windows = [held.tile([P, STORE], F32, name=f"window{b}") for b in range(C_BLOCKS)]
 
-        nc.scalar.dma_start(w1_sb[:], w1.rearrange("(p t) c -> p t c", t=F_TILES))
+        for b in range(C_BLOCKS):
+            nc.scalar.dma_start(w1_sb[b][:], w1[:, b * P : (b + 1) * P].rearrange("(p t) c -> p t c", t=F_TILES))
         nc.sync.dma_start(bias_cols[:], b1.rearrange("(b p) o -> p (b o)", p=P))
         nc.sync.dma_start(adj_sb[:], adj)
         nc.sync.dma_start(x_sb[:], x.rearrange("(p t) k -> p t k", t=F_TILES))
@@ -56,12 +57,11 @@ def tile_gcnlayer_kernel(tc, x, w1, b1, adj, base, offs, out):
         bias_low = held.tile([P, C_BLOCKS], BF16, name="bias_low")
         nc.vector.tensor_tensor(bias_low[:], bias_cols[:], bias_high[:], SUBTRACT)
         def scaled_features(b):
-            block = slice(b * P, (b + 1) * P)
             h_t = psum.tile([P, P], F32, name=f"h_t{b}")
             nc.tensor.matmul(h_t[:], bias_high[:, b : b + 1].to_broadcast([P, P]), identity[:], start=True, stop=False)
             nc.tensor.matmul(h_t[:], bias_low[:, b : b + 1].to_broadcast([P, P]), identity[:], start=False, stop=False)
             for t in range(F_TILES):
-                nc.tensor.matmul(h_t[:], x_sb[:, t, :], w1_sb[:, t, block], start=False, stop=(t == F_TILES - 1))
+                nc.tensor.matmul(h_t[:], x_sb[:, t, :], w1_sb[b][:, t, :], start=False, stop=(t == F_TILES - 1))
             hs_t_block = held.tile([P, P], BF16, name=f"hs_t{b}")
             nc.vector.tensor_scalar_mul(hs_t_block[:], h_t[:], dinv_own[:])
             return hs_t_block

@@ -4,7 +4,7 @@ from concourse.masks import make_identity
 BF16, F32, U16 = mybir.dt.bfloat16, mybir.dt.float32, mybir.dt.uint16
 MULT, SUBTRACT = mybir.AluOpType.mult, mybir.AluOpType.subtract
 RSQRT_OF_ABS = mybir.ActivationFunctionType.Abs_reciprocal_sqrt
-ALONG_ROW = mybir.AxisListType.X
+COPY = mybir.ActivationFunctionType.Copy
 
 P = 128
 FEATURES, CHANNELS, NODES, STORE = 256, 256, 128, 512
@@ -24,13 +24,13 @@ def tile_gcnlayer_kernel(tc, x, w1, b1, adj, base, offs, out):
         adj_sb = held.tile([P, NODES], BF16, name="adj_sb")
         x_sb = held.tile([P, F_TILES, NODES], BF16, name="x_sb")
         w1_sb = [held.tile([P, F_TILES, P], BF16, name=f"w1_sb{b}") for b in range(C_BLOCKS)]
-        bias_cols = held.tile([P, C_BLOCKS], F32, name="bias_cols")
+        bias_row = held.tile([1, CHANNELS], F32, name="bias_row")
         offsets = held.tile([P, NODES // 16], U16, name="offsets")
         windows = [held.tile([P, STORE], F32, name=f"window{b}") for b in range(C_BLOCKS)]
 
         for b in range(C_BLOCKS):
             nc.scalar.dma_start(w1_sb[b][:], w1[:, b * P : (b + 1) * P].rearrange("(p t) c -> p t c", t=F_TILES))
-        nc.sync.dma_start(bias_cols[:], b1.rearrange("(b p) o -> p (b o)", p=P))
+        nc.sync.dma_start(bias_row[:], b1.rearrange("c o -> o c"))
         nc.sync.dma_start(adj_sb[:], adj)
         nc.sync.dma_start(x_sb[:], x.rearrange("(p t) k -> p t k", t=F_TILES))
         for b in range(C_BLOCKS):
@@ -48,20 +48,28 @@ def tile_gcnlayer_kernel(tc, x, w1, b1, adj, base, offs, out):
         nc.vector.memset(ones[:], 1.0)
 
         degree_own = held.tile([P, 1], F32, name="degree_own")
-        nc.vector.reduce_sum(degree_own[:], adj_sb[:], axis=ALONG_ROW)
+        adj_copy = held.tile([P, NODES], BF16, name="adj_copy")
+        nc.scalar.activation(adj_copy[:], adj_sb[:], COPY, accum_out=degree_own[:])
         dinv_own = held.tile([P, 1], F32, name="dinv_own")
         nc.scalar.activation(dinv_own[:], degree_own[:], RSQRT_OF_ABS, bias=1.0)
 
-        bias_high = held.tile([P, C_BLOCKS], BF16, name="bias_high")
-        nc.vector.tensor_copy(bias_high[:], bias_cols[:])
-        bias_low = held.tile([P, C_BLOCKS], BF16, name="bias_low")
-        nc.vector.tensor_tensor(bias_low[:], bias_cols[:], bias_high[:], SUBTRACT)
+        bias_parts = []
+        for b in range(C_BLOCKS):
+            parts = held.tile([P, 2, P], BF16, name=f"bias_parts{b}")
+            nc.gpsimd.memset(parts[:], 0.0)
+            bias_parts.append(parts)
+        for b in range(C_BLOCKS):
+            bias = bias_row[:, b * P : (b + 1) * P]
+            high, rest = bias_parts[b][0:1, 0, :], bias_parts[b][0:1, 1, :]
+            nc.vector.tensor_copy(high, bias)
+            nc.vector.tensor_tensor(rest, bias, high, SUBTRACT)
+
         def scaled_features(b):
             h_t = psum.tile([P, P], F32, name=f"h_t{b}")
-            nc.tensor.matmul(h_t[:], bias_high[:, b : b + 1].to_broadcast([P, P]), identity[:], start=True, stop=False)
-            nc.tensor.matmul(h_t[:], bias_low[:, b : b + 1].to_broadcast([P, P]), identity[:], start=False, stop=False)
             for t in range(F_TILES):
-                nc.tensor.matmul(h_t[:], x_sb[:, t, :], w1_sb[b][:, t, :], start=False, stop=(t == F_TILES - 1))
+                nc.tensor.matmul(h_t[:], x_sb[:, t, :], w1_sb[b][:, t, :], start=(t == 0), stop=False)
+            nc.tensor.matmul(h_t[:], ones[:], bias_parts[b][:, 0, :], start=False, stop=False)
+            nc.tensor.matmul(h_t[:], ones[:], bias_parts[b][:, 1, :], start=False, stop=True)
             hs_t_block = held.tile([P, P], BF16, name=f"hs_t{b}")
             nc.vector.tensor_scalar_mul(hs_t_block[:], h_t[:], dinv_own[:])
             return hs_t_block

@@ -4,7 +4,7 @@ from concourse.masks import make_identity
 BF16, F32, U16 = mybir.dt.bfloat16, mybir.dt.float32, mybir.dt.uint16
 MULT, SUBTRACT = mybir.AluOpType.mult, mybir.AluOpType.subtract
 RSQRT_OF_ABS = mybir.ActivationFunctionType.Abs_reciprocal_sqrt
-COPY = mybir.ActivationFunctionType.Copy
+ALONG_ROW = mybir.AxisListType.X
 
 P = 128
 FEATURES, CHANNELS, NODES, STORE = 256, 256, 128, 512
@@ -47,29 +47,23 @@ def tile_gcnlayer_kernel(tc, x, w1, b1, adj, base, offs, out):
         ones = held.tile([P, P], BF16, name="ones")
         nc.vector.memset(ones[:], 1.0)
 
+        bias_parts = held.tile([P, 2, CHANNELS], BF16, name="bias_parts")
+        nc.gpsimd.memset(bias_parts[:], 0.0)
+        bias_high, bias_rest = bias_parts[0:1, 0, :], bias_parts[0:1, 1, :]
+        nc.vector.tensor_copy(bias_high, bias_row[:])
+        nc.vector.tensor_tensor(bias_rest, bias_row[:], bias_high, SUBTRACT)
+
         degree_own = held.tile([P, 1], F32, name="degree_own")
-        adj_copy = held.tile([P, NODES], BF16, name="adj_copy")
-        nc.scalar.activation(adj_copy[:], adj_sb[:], COPY, accum_out=degree_own[:])
+        nc.vector.reduce_sum(degree_own[:], adj_sb[:], axis=ALONG_ROW)
         dinv_own = held.tile([P, 1], F32, name="dinv_own")
         nc.scalar.activation(dinv_own[:], degree_own[:], RSQRT_OF_ABS, bias=1.0)
 
-        bias_parts = []
-        for b in range(C_BLOCKS):
-            parts = held.tile([P, 2, P], BF16, name=f"bias_parts{b}")
-            nc.gpsimd.memset(parts[:], 0.0)
-            bias_parts.append(parts)
-        for b in range(C_BLOCKS):
-            bias = bias_row[:, b * P : (b + 1) * P]
-            high, rest = bias_parts[b][0:1, 0, :], bias_parts[b][0:1, 1, :]
-            nc.vector.tensor_copy(high, bias)
-            nc.vector.tensor_tensor(rest, bias, high, SUBTRACT)
-
         def scaled_features(b):
             h_t = psum.tile([P, P], F32, name=f"h_t{b}")
+            for part in range(2):
+                nc.tensor.matmul(h_t[:], ones[:], bias_parts[:, part, b * P : (b + 1) * P], start=(part == 0), stop=False)
             for t in range(F_TILES):
-                nc.tensor.matmul(h_t[:], x_sb[:, t, :], w1_sb[b][:, t, :], start=(t == 0), stop=False)
-            nc.tensor.matmul(h_t[:], ones[:], bias_parts[b][:, 0, :], start=False, stop=False)
-            nc.tensor.matmul(h_t[:], ones[:], bias_parts[b][:, 1, :], start=False, stop=True)
+                nc.tensor.matmul(h_t[:], x_sb[:, t, :], w1_sb[b][:, t, :], start=False, stop=(t == F_TILES - 1))
             hs_t_block = held.tile([P, P], BF16, name=f"hs_t{b}")
             nc.vector.tensor_scalar_mul(hs_t_block[:], h_t[:], dinv_own[:])
             return hs_t_block

@@ -2,9 +2,9 @@ import concourse.mybir as mybir
 from concourse.masks import make_identity
 
 BF16, F32, U16 = mybir.dt.bfloat16, mybir.dt.float32, mybir.dt.uint16
-MULT, SUBTRACT = mybir.AluOpType.mult, mybir.AluOpType.subtract
+MULT, ADD = mybir.AluOpType.mult, mybir.AluOpType.add
 RSQRT_OF_ABS = mybir.ActivationFunctionType.Abs_reciprocal_sqrt
-ALONG_ROW = mybir.AxisListType.X
+COPY = mybir.ActivationFunctionType.Copy
 
 P = 128
 FEATURES, CHANNELS, NODES, STORE = 256, 256, 128, 512
@@ -24,15 +24,18 @@ def tile_gcnlayer_kernel(tc, x, w1, b1, adj, base, offs, out):
         adj_sb = held.tile([P, NODES], BF16, name="adj_sb")
         x_sb = held.tile([P, F_TILES, NODES], BF16, name="x_sb")
         w1_sb = [held.tile([P, F_TILES, P], BF16, name=f"w1_sb{b}") for b in range(C_BLOCKS)]
-        bias_row = held.tile([1, CHANNELS], F32, name="bias_row")
+        bias_rows = held.tile([2, CHANNELS], F32, name="bias_rows")
         offsets = held.tile([P, NODES // 16], U16, name="offsets")
         windows = [held.tile([P, STORE], F32, name=f"window{b}") for b in range(C_BLOCKS)]
 
-        for b in range(C_BLOCKS):
-            nc.scalar.dma_start(w1_sb[b][:], w1[:, b * P : (b + 1) * P].rearrange("(p t) c -> p t c", t=F_TILES))
-        nc.sync.dma_start(bias_row[:], b1.rearrange("c o -> o c"))
+        def load_w1(queue, b):
+            queue.dma_start(w1_sb[b][:], w1[:, b * P : (b + 1) * P].rearrange("(p t) c -> p t c", t=F_TILES))
+
+        load_w1(nc.scalar, 0)
+        nc.sync.dma_start(bias_rows[:], b1.rearrange("c o -> (c o)").partition_broadcast(2))
         nc.sync.dma_start(adj_sb[:], adj)
         nc.sync.dma_start(x_sb[:], x.rearrange("(p t) k -> p t k", t=F_TILES))
+        load_w1(nc.sync, 1)
         for b in range(C_BLOCKS):
             nc.sync.dma_start(windows[b][:], base[b * P : (b + 1) * P, :])
         nc.sync.dma_start(offsets[:], offs)
@@ -47,38 +50,38 @@ def tile_gcnlayer_kernel(tc, x, w1, b1, adj, base, offs, out):
         ones = held.tile([P, P], BF16, name="ones")
         nc.vector.memset(ones[:], 1.0)
 
-        bias_parts = held.tile([P, 2, CHANNELS], BF16, name="bias_parts")
+        bias_parts = held.tile([P, CHANNELS], BF16, name="bias_parts")
         nc.gpsimd.memset(bias_parts[:], 0.0)
-        bias_high, bias_rest = bias_parts[0:1, 0, :], bias_parts[0:1, 1, :]
-        nc.vector.tensor_copy(bias_high, bias_row[:])
-        nc.vector.tensor_tensor(bias_rest, bias_row[:], bias_high, SUBTRACT)
+        minus_mask = held.tile([2, 1], F32, name="minus_mask")
+        nc.vector.memset(minus_mask[:], -1.0)
+        nc.vector.memset(minus_mask[0:1, :], 0.0)
+        bias_rounded = held.tile([2, CHANNELS], BF16, name="bias_rounded")
+        block_columns = [slice(b * P, (b + 1) * P) for b in range(C_BLOCKS)]
+        for columns in block_columns:
+            nc.vector.tensor_copy(bias_rounded[:, columns], bias_rows[:, columns])
+        for columns in block_columns:
+            nc.vector.scalar_tensor_tensor(bias_parts[0:2, columns], bias_rounded[:, columns], minus_mask[:], bias_rows[:, columns], MULT, ADD)
 
-        degree_own = held.tile([P, 1], F32, name="degree_own")
-        nc.vector.reduce_sum(degree_own[:], adj_sb[:], axis=ALONG_ROW)
-        dinv_own = held.tile([P, 1], F32, name="dinv_own")
-        nc.scalar.activation(dinv_own[:], degree_own[:], RSQRT_OF_ABS, bias=1.0)
+        sums = psum.tile([P, NODES + 1], F32, name="sums")
+        nc.tensor.matmul(sums[:, NODES:], adj_sb[:], ones[:, 0:1], start=True, stop=True)
+        nc.tensor.matmul(sums[:, 0:NODES], ones[:], adj_sb[:], start=True, stop=True)
+        dinv = held.tile([P, NODES + 1], F32, name="dinv")
+        nc.scalar.activation(dinv[:], sums[:], RSQRT_OF_ABS, bias=1.0)
+        dinv_row, dinv_own = dinv[:, 0:NODES], dinv[:, NODES:]
 
-        def scaled_features(b):
+        def features(b):
             h_t = psum.tile([P, P], F32, name=f"h_t{b}")
-            for part in range(2):
-                nc.tensor.matmul(h_t[:], ones[:], bias_parts[:, part, b * P : (b + 1) * P], start=(part == 0), stop=False)
             for t in range(F_TILES):
-                nc.tensor.matmul(h_t[:], x_sb[:, t, :], w1_sb[b][:, t, :], start=False, stop=(t == F_TILES - 1))
-            hs_t_block = held.tile([P, P], BF16, name=f"hs_t{b}")
-            nc.vector.tensor_scalar_mul(hs_t_block[:], h_t[:], dinv_own[:])
-            return hs_t_block
+                nc.tensor.matmul(h_t[:], x_sb[:, t, :], w1_sb[b][:, t, :], start=(t == 0), stop=False)
+            nc.tensor.matmul(h_t[:], ones[:], bias_parts[:, block_columns[b]], start=False, stop=True)
+            return h_t
 
-        hs_t = [scaled_features(0)]
-
-        sums_row = psum.tile([P, NODES], F32, name="sums_row")
-        nc.tensor.matmul(sums_row[:], ones[:], adj_sb[:], start=True, stop=True)
-        dinv_row = held.tile([P, NODES], F32, name="dinv_row")
-        nc.scalar.activation(dinv_row[:], sums_row[:], RSQRT_OF_ABS, bias=1.0)
-
-        hs_t.extend(scaled_features(b) for b in range(1, C_BLOCKS))
+        hs_t = [held.tile([P, P], BF16, name=f"hs_t{b}") for b in range(C_BLOCKS)]
+        nc.vector.tensor_scalar_mul(hs_t[0][:], features(0)[:], dinv_own)
+        nc.scalar.activation(hs_t[1][:], features(1)[:], COPY, scale=dinv_own)
 
         for b in range(C_BLOCKS):
-            agg = psum.tile([P, NODES], F32, name=f"agg{b}")
+            agg = psum.tile([P, NODES], F32, name=f"agg{b}", tag="agg")
             nc.tensor.matmul(agg[:], hs_t[b][:], adj_sb[:], start=True, stop=False)
             nc.tensor.matmul(agg[:], hs_t[b][:], identity[:], start=False, stop=True)
             agg_sb = held.tile([P, NODES], F32, name=f"agg_sb{b}")
@@ -86,6 +89,5 @@ def tile_gcnlayer_kernel(tc, x, w1, b1, adj, base, offs, out):
                 nc.vector.tensor_copy(agg_sb[:], agg[:])
             else:
                 nc.scalar.copy(agg_sb[:], agg[:])
-            nc.vector.tensor_tensor(windows[b][:].indirect(offsets[:]), agg_sb[:], dinv_row[:], MULT)
-            store_queue = nc.sync if b == C_BLOCKS - 1 else nc.scalar
-            store_queue.dma_start(out[b * P : (b + 1) * P, :], windows[b][:])
+            nc.vector.tensor_tensor(windows[b][:].indirect(offsets[:]), agg_sb[:], dinv_row, MULT)
+            nc.sync.dma_start(out[b * P : (b + 1) * P, :], windows[b][:])

@@ -36,9 +36,9 @@ def tile_gcnlayer_kernel(tc, x, w1, b1, adj, base, offs, out):
         nc.sync.dma_start(adj_sb[:], adj)
         nc.sync.dma_start(x_sb[:], x.rearrange("(p t) k -> p t k", t=F_TILES))
         load_w1(nc.sync, 1)
-        for b in range(C_BLOCKS):
-            nc.sync.dma_start(windows[b][:], base[b * P : (b + 1) * P, :])
+        nc.sync.dma_start(windows[0][:], base[0:P, :])
         nc.sync.dma_start(offsets[:], offs)
+        nc.sync.dma_start(windows[1][:], base[P : 2 * P, :])
 
         idle_work = held.tile([P, 1], BF16, name="idle_work")
         nc.gpsimd.memset(idle_work[:], 0.0)

@@ -2,7 +2,7 @@ import concourse.mybir as mybir
 from concourse.masks import make_identity
 
 BF16, F32, U16 = mybir.dt.bfloat16, mybir.dt.float32, mybir.dt.uint16
-MULT, ADD = mybir.AluOpType.mult, mybir.AluOpType.add
+MULT, SUBTRACT = mybir.AluOpType.mult, mybir.AluOpType.subtract
 RSQRT_OF_ABS = mybir.ActivationFunctionType.Abs_reciprocal_sqrt
 COPY = mybir.ActivationFunctionType.Copy
 
@@ -24,15 +24,15 @@ def tile_gcnlayer_kernel(tc, x, w1, b1, adj, base, offs, out):
         adj_sb = held.tile([P, NODES], BF16, name="adj_sb")
         x_sb = held.tile([P, F_TILES, NODES], BF16, name="x_sb")
         w1_sb = [held.tile([P, F_TILES, P], BF16, name=f"w1_sb{b}") for b in range(C_BLOCKS)]
-        bias_rows = held.tile([2, CHANNELS], F32, name="bias_rows")
+        bias_row = held.tile([1, CHANNELS], F32, name="bias_row")
         offsets = held.tile([P, NODES // 16], U16, name="offsets")
         windows = [held.tile([P, STORE], F32, name=f"window{b}") for b in range(C_BLOCKS)]
 
         def load_w1(queue, b):
             queue.dma_start(w1_sb[b][:], w1[:, b * P : (b + 1) * P].rearrange("(p t) c -> p t c", t=F_TILES))
 
+        nc.scalar.dma_start(bias_row[:], b1.rearrange("c o -> o c"))
         load_w1(nc.scalar, 0)
-        nc.sync.dma_start(bias_rows[:], b1.rearrange("c o -> (c o)").partition_broadcast(2))
         nc.sync.dma_start(adj_sb[:], adj)
         nc.sync.dma_start(x_sb[:], x.rearrange("(p t) k -> p t k", t=F_TILES))
         load_w1(nc.sync, 1)
@@ -50,17 +50,13 @@ def tile_gcnlayer_kernel(tc, x, w1, b1, adj, base, offs, out):
         ones = held.tile([P, P], BF16, name="ones")
         nc.vector.memset(ones[:], 1.0)
 
-        bias_parts = held.tile([P, CHANNELS], BF16, name="bias_parts")
+        bias_parts = held.tile([P, 2, CHANNELS], BF16, name="bias_parts")
         nc.gpsimd.memset(bias_parts[:], 0.0)
-        minus_mask = held.tile([2, 1], F32, name="minus_mask")
-        nc.vector.memset(minus_mask[:], -1.0)
-        nc.vector.memset(minus_mask[0:1, :], 0.0)
-        bias_rounded = held.tile([2, CHANNELS], BF16, name="bias_rounded")
         block_columns = [slice(b * P, (b + 1) * P) for b in range(C_BLOCKS)]
         for columns in block_columns:
-            nc.vector.tensor_copy(bias_rounded[:, columns], bias_rows[:, columns])
+            nc.vector.tensor_copy(bias_parts[0:1, 0, columns], bias_row[:, columns])
         for columns in block_columns:
-            nc.vector.scalar_tensor_tensor(bias_parts[0:2, columns], bias_rounded[:, columns], minus_mask[:], bias_rows[:, columns], MULT, ADD)
+            nc.vector.tensor_tensor(bias_parts[0:1, 1, columns], bias_row[:, columns], bias_parts[0:1, 0, columns], SUBTRACT)
 
         sums = psum.tile([P, NODES + 1], F32, name="sums")
         nc.tensor.matmul(sums[:, NODES:], adj_sb[:], ones[:, 0:1], start=True, stop=True)
@@ -71,9 +67,10 @@ def tile_gcnlayer_kernel(tc, x, w1, b1, adj, base, offs, out):
 
         def features(b):
             h_t = psum.tile([P, P], F32, name=f"h_t{b}")
+            nc.tensor.matmul(h_t[:], ones[:], bias_parts[:, 0, block_columns[b]], start=True, stop=False)
             for t in range(F_TILES):
-                nc.tensor.matmul(h_t[:], x_sb[:, t, :], w1_sb[b][:, t, :], start=(t == 0), stop=False)
-            nc.tensor.matmul(h_t[:], ones[:], bias_parts[:, block_columns[b]], start=False, stop=True)
+                nc.tensor.matmul(h_t[:], x_sb[:, t, :], w1_sb[b][:, t, :], start=False, stop=False)
+            nc.tensor.matmul(h_t[:], ones[:], bias_parts[:, 1, block_columns[b]], start=False, stop=True)
             return h_t
 
         hs_t = [held.tile([P, P], BF16, name=f"hs_t{b}") for b in range(C_BLOCKS)]

@@ -10,7 +10,7 @@ P = 128
 FEATURES, CHANNELS, NODES, STORE = 256, 256, 128, 512
 F_TILES = FEATURES // P
 C_BLOCKS = CHANNELS // P
-WARM_UP_MATMULS = 16
+WARM_UP_MATMULS = 12
 
 FLOPS = 2 * FEATURES * CHANNELS * NODES + 2 * NODES * NODES * CHANNELS
 

@@ -10,7 +10,7 @@ P = 128
 FEATURES, CHANNELS, NODES, STORE = 256, 256, 128, 512
 F_TILES = FEATURES // P
 C_BLOCKS = CHANNELS // P
-WARM_UP_MATMULS = 12
+WARM_UP_MATMULS = 9
 
 FLOPS = 2 * FEATURES * CHANNELS * NODES + 2 * NODES * NODES * CHANNELS
 

import concourse.mybir as mybir
from concourse.masks import make_identity

BF16, F32, U16 = mybir.dt.bfloat16, mybir.dt.float32, mybir.dt.uint16
MULT, SUBTRACT = mybir.AluOpType.mult, mybir.AluOpType.subtract
RSQRT_OF_ABS = mybir.ActivationFunctionType.Abs_reciprocal_sqrt
COPY = mybir.ActivationFunctionType.Copy

P = 128
FEATURES, CHANNELS, NODES, STORE = 256, 256, 128, 512
F_TILES = FEATURES // P
C_BLOCKS = CHANNELS // P
WARM_UP_MATMULS = 9

FLOPS = 2 * FEATURES * CHANNELS * NODES + 2 * NODES * NODES * CHANNELS


def tile_gcnlayer_kernel(tc, x, w1, b1, adj, base, offs, out):
    nc = tc.nc
    with (
        tc.tile_pool(name="held", bufs=1) as held,
        tc.psum_pool(name="psum", bufs=1) as psum,
    ):
        adj_sb = held.tile([P, NODES], BF16, name="adj_sb")
        x_sb = held.tile([P, F_TILES, NODES], BF16, name="x_sb")
        w1_sb = [held.tile([P, F_TILES, P], BF16, name=f"w1_sb{b}") for b in range(C_BLOCKS)]
        bias_row = held.tile([1, CHANNELS], F32, name="bias_row")
        offsets = held.tile([P, NODES // 16], U16, name="offsets")
        windows = [held.tile([P, STORE], F32, name=f"window{b}") for b in range(C_BLOCKS)]

        def load_w1(queue, b):
            queue.dma_start(w1_sb[b][:], w1[:, b * P : (b + 1) * P].rearrange("(p t) c -> p t c", t=F_TILES))

        nc.scalar.dma_start(bias_row[:], b1.rearrange("c o -> o c"))
        load_w1(nc.scalar, 0)
        nc.sync.dma_start(adj_sb[:], adj)
        nc.sync.dma_start(x_sb[:], x.rearrange("(p t) k -> p t k", t=F_TILES))
        load_w1(nc.sync, 1)
        nc.sync.dma_start(windows[0][:], base[0:P, :])
        nc.sync.dma_start(offsets[:], offs)
        nc.sync.dma_start(windows[1][:], base[P : 2 * P, :])

        idle_work = held.tile([P, 1], BF16, name="idle_work")
        nc.gpsimd.memset(idle_work[:], 0.0)
        warm_up = psum.tile([P, P], F32, name="warm_up")
        for i in range(WARM_UP_MATMULS):
            nc.tensor.matmul(warm_up[:], idle_work[:].to_broadcast([P, P]), idle_work[:].to_broadcast([P, P]), start=True, stop=True)
        identity = held.tile([P, P], BF16, name="identity")
        make_identity(nc, identity[:])
        ones = held.tile([P, P], BF16, name="ones")
        nc.vector.memset(ones[:], 1.0)

        bias_parts = held.tile([P, 2, CHANNELS], BF16, name="bias_parts")
        nc.gpsimd.memset(bias_parts[:], 0.0)
        block_columns = [slice(b * P, (b + 1) * P) for b in range(C_BLOCKS)]
        for columns in block_columns:
            nc.vector.tensor_copy(bias_parts[0:1, 0, columns], bias_row[:, columns])
        for columns in block_columns:
            nc.vector.tensor_tensor(bias_parts[0:1, 1, columns], bias_row[:, columns], bias_parts[0:1, 0, columns], SUBTRACT)

        sums = psum.tile([P, NODES + 1], F32, name="sums")
        nc.tensor.matmul(sums[:, NODES:], adj_sb[:], ones[:, 0:1], start=True, stop=True)
        nc.tensor.matmul(sums[:, 0:NODES], ones[:], adj_sb[:], start=True, stop=True)
        dinv = held.tile([P, NODES + 1], F32, name="dinv")
        nc.scalar.activation(dinv[:], sums[:], RSQRT_OF_ABS, bias=1.0)
        dinv_row, dinv_own = dinv[:, 0:NODES], dinv[:, NODES:]

        def features(b):
            h_t = psum.tile([P, P], F32, name=f"h_t{b}")
            nc.tensor.matmul(h_t[:], ones[:], bias_parts[:, 0, block_columns[b]], start=True, stop=False)
            for t in range(F_TILES):
                nc.tensor.matmul(h_t[:], x_sb[:, t, :], w1_sb[b][:, t, :], start=False, stop=False)
            nc.tensor.matmul(h_t[:], ones[:], bias_parts[:, 1, block_columns[b]], start=False, stop=True)
            return h_t

        hs_t = [held.tile([P, P], BF16, name=f"hs_t{b}") for b in range(C_BLOCKS)]
        nc.vector.tensor_scalar_mul(hs_t[0][:], features(0)[:], dinv_own)
        nc.scalar.activation(hs_t[1][:], features(1)[:], COPY, scale=dinv_own)

        for b in range(C_BLOCKS):
            agg = psum.tile([P, NODES], F32, name=f"agg{b}", tag="agg")
            nc.tensor.matmul(agg[:], hs_t[b][:], adj_sb[:], start=True, stop=False)
            nc.tensor.matmul(agg[:], hs_t[b][:], identity[:], start=False, stop=True)
            agg_sb = held.tile([P, NODES], F32, name=f"agg_sb{b}")
            if b == 0:
                nc.vector.tensor_copy(agg_sb[:], agg[:])
            else:
                nc.scalar.copy(agg_sb[:], agg[:])
            nc.vector.tensor_tensor(windows[b][:].indirect(offsets[:]), agg_sb[:], dinv_row, MULT)
            nc.sync.dma_start(out[b * P : (b + 1) * P, :], windows[b][:])
